import numpy as np
import ml_dtypes


def mxq(x, axis, fmt="e4m3"):
    dtype, down = {"e4m3": (ml_dtypes.float8_e4m3fn, 7), "e5m2": (ml_dtypes.float8_e5m2, 14)}[fmt]
    v = np.moveaxis(np.asarray(x, np.float32).astype(ml_dtypes.bfloat16).astype(np.float64), axis, -1)
    blocks = v.reshape(v.shape[:-1] + (-1, 32))
    amax = np.abs(blocks).max(-1, keepdims=True)
    byte = np.maximum(np.where(amax > 0, np.frexp(amax)[1] - 1 + 127, 0) - down, 1)
    scale = np.exp2(byte - 127.0)
    codes = (blocks / scale).astype(np.float32).astype(dtype).astype(np.float64)
    return np.moveaxis((codes * scale).reshape(v.shape), -1, axis)


WIDE = False


def mx_kscale(k):
    if not WIDE:
        return np.ones(k)
    levels = np.array([18, -18])
    if k % 512:
        return np.exp2(np.random.permutation(np.resize(levels, k // 32))).repeat(32)
    a = np.empty((k // 512, 16))
    for p in range(k // 512):
        a[p, :8] = np.random.permutation(np.resize(levels, 8))
        for g in range(8):
            far = levels[np.abs(levels - a[p, g]) >= 10]
            a[p, g + 8] = far[np.random.randint(len(far))]
    return np.exp2(a.ravel()).repeat(32)


BF16 = ml_dtypes.bfloat16


def bf(x):
    return np.asarray(x, np.float32).astype(BF16)


def f64(x):
    return np.asarray(x).astype(np.float64)


B, I, H = 1024, 1024, 512


def sigmoid(v):
    return 1.0 / (1.0 + np.exp(-v))


def setup_inputs():
    s = mx_kscale(B)[:, None]
    u = mx_kscale(H)
    x0 = bf(np.random.standard_normal((B, I)))
    h = bf(np.random.standard_normal((B, H)))
    c = bf(np.random.standard_normal((B, H)))
    w0 = bf(np.random.standard_normal((4, H, I)) * 0.8 / np.sqrt(I))
    Wh = bf(np.random.standard_normal((4, H, H)) * 0.8 / np.sqrt(H))
    bx = bf(np.random.standard_normal((4, H)) * 0.3)
    bh = bf(np.random.standard_normal((4, H)) * 0.3)
    e = np.exp2(np.random.randint(-6, 1, (B, 1)))
    g0 = bf(np.random.standard_normal((B, H)) * e * 8.0 / s * u)
    g1 = bf(np.random.standard_normal((B, H)) * e * 8.0 / s * u)
    z = (f64(x0) @ f64(w0).reshape(4 * H, I).T + f64(bx).reshape(-1)
         + f64(h) @ f64(Wh).reshape(4 * H, H).T + f64(bh).reshape(-1))
    c_new = sigmoid(z[:, H:2 * H]) * f64(c) + sigmoid(z[:, :H]) * np.tanh(z[:, 2 * H:3 * H])
    return {"x": bf(f64(x0) * s), "h": h, "c": c,
            "Wx": bf(f64(w0) / u[:, None]), "Wh": Wh, "bx": bx, "bh": bh,
            "z": np.asarray(z, np.float32), "c_new": np.asarray(c_new, np.float32),
            "grad_0": g0, "grad_1": g1}


def reference(x, h, c, Wx, Wh, bx, bh, z, c_new, grad_0, grad_1):
    zf = f64(z)
    i = sigmoid(zf[:, :H])
    f = sigmoid(zf[:, H:2 * H])
    gc = np.tanh(zf[:, 2 * H:3 * H])
    o = sigmoid(zf[:, 3 * H:])
    tc = np.tanh(f64(c_new))
    g0 = f64(grad_0)
    dc = f64(grad_1) + g0 * o * (1.0 - tc * tc)
    dz = np.concatenate([dc * gc * i * (1.0 - i),
                         dc * f64(c) * f * (1.0 - f),
                         dc * i * (1.0 - gc * gc),
                         g0 * tc * o * (1.0 - o)], axis=1)
    wx = f64(Wx).reshape(4 * H, I)
    dx = mxq(dz, 1, "e5m2") @ mxq(wx, 0, "e4m3")
    dw = mxq(dz, 0, "e5m2").T @ mxq(f64(x), 0, "e4m3")
    return dx, dw.reshape(4, H, I)

@@ -1,0 +1,319 @@
+from contextlib import ExitStack
+
+import concourse.mybir as mybir
+from concourse.masks import make_identity
+
+B, I, H, GATES = 1024, 1024, 512, 4
+FLOPS = 2 * 2 * B * GATES * H * I
+BYTES = 2 * (B * I + B * H + GATES * H * I + 2 * B * H) + 4 * (B * GATES * H + B * H) + 4 * (B * I + GATES * H * I)
+
+F32 = mybir.dt.float32
+BF16 = mybir.dt.bfloat16
+U32 = mybir.dt.uint32
+U8 = mybir.dt.uint8
+E4M3 = mybir.dt.float8_e4m3fn_x4
+E5M2 = mybir.dt.float8_e5m2_x4
+ACT = mybir.ActivationFunctionType
+ALU = mybir.AluOpType
+
+P = 128
+J = 4
+TOK = P * J
+BANK = 512
+HALF = H // 2
+MODES = "BBAB"
+LAST = 2
+STEPS = """
+Lx1 Lx01 Lz03a xil10/V xil11/S Lz03b xil01/V Lg00 s3a0 xq11 Lw0 xq10 xq01 s30
+m0 Lcn0 wil01/V wil00/S Lw1 a30 tc0 Lz13 wq00 wq01 wil11/V wil10/S Lg11 dz30a
+Lg01 s31 Lz11 wq11 wq10 dz30b m1 Lcn1 sqc0 T03 qt03a t11 Lc1 a31
+Lz02 tc1 q0 Lz10 sq11 dz31a qt03b Lx00 dz31b t20 Lw3 b11 T13 sqc1
+qt13a Lg10 tcp13a/V Lz00 tcp13b/S qt13b q1 wil31/S Lz12 qf13 ndc1 xil00/S Lc0 ndc0
+Lw2 wil30/S dz11a s01 wq30 xq00 wq31 O1300 dz11b O1330 t21 O1320 O1331 x21
+Lz01 T11 e1300/S e1331/S O1321 qt11a tcp11a/S O1301 b01 e1301/S O1310 wil21/S st130 O1311
+qt11b e1321/V dz01a sqg1 wq21 dz01b tcp11b/V e1310/S t10 T10 dz21a qf11 tcp10a/S dz21b
+il12a/V tcp10b/S T12 e1320/V sq10 qf10 st132 tcp12a/V O0p120 qt10a e1330/V O0p100 qt10b tcp12b/S
+st133 b10 O0p121 e1311/S wil20/S st131 O0p101 O0p130 qf12 dz10a O0121 O0101 s00 O0p131
+wq20 O0131 dz10b O0130 O0100 O0120 e0101/S e0100/V e0120/S O0p110 x20 st010 e0130/S T01
+e0131/S e0121/S st013 O0110 tcp03a/S O0p111 qt01a b00 st012 O1100 tcp01b/S O1110 O1101 e1100/S
+qt01b e1110/S O1111 dz00a e1101/S O1130 O0111 tcp01a/S st110 O1131 e1111/V O1120 dz00b e1130/S
+st111 e1131/S O1121 e0110/V e1120/S st113 T00 e1121/S e0111/V qt12a sqg0 st112 qt00a tcp00b/V
+O1000 st011 O1010 qt00b O1001 qf01 e1000/S O1011 dz20a e1010/S O1020 e1001/S O1030 dz20b
+e1011/S st100 O1021 e1020/S O1031 il02a/V tcp00a/S st101 T02 e1021/V e1031/S qt02a st102 qf00
+tcp03b/S O1210 tcp02a/V O1200 e1210/V il12b/S O1211 qf03 O1201 tcp02b/V O0p030 e1211/S e1201/V e1200/S
+st121 O0p010 qt12b qf02 O0p031 il02b/V st120 O0010 e1030/V O0p011 qt02b st103 e0010/V O0031
+O0011 O1230 e0031/S e0011/V O0030 O1231 e1230/V st001 e0030/S O0p020 e1231/S st003 O1220 O0020
+O1221 e1220/S st123 O0p021 e0020/S e1221/S O0p000 st122 O0021 O0p001 e0021/S O0000 st002 O0001
+e0000/V e0001/S st000
+""".split()
+
+
+def tile_lstmcell_v_kernel(tc, x, h, c, Wx, Wh, bx, bh, z, c_new, grad_0, grad_1, out_0, out_1):
+    nc = tc.nc
+    V, S, T = nc.vector, nc.scalar, nc.tensor
+
+    def tokens(t, g, cols=slice(None)):
+        return t[g * TOK:(g + 1) * TOK, cols].rearrange("(p j) w -> p j w", j=J)
+
+    halves = (slice(0, HALF), slice(HALF, H))
+    wide = (slice(0, BANK), slice(BANK, 2 * BANK))
+
+    with ExitStack() as ctx:
+        pool = lambda name, bufs: ctx.enter_context(tc.tile_pool(name=name, bufs=bufs))
+        const = pool("const", 1)
+        zp = pool("zp", 5)
+        cnp = pool("cnp", 2)
+        rawp = pool("rawp", 3)
+        mp = pool("mp", 2)
+        in4 = pool("in4", 4)
+        dzp = pool("dzp", 3)
+        ilp = pool("ilp", 4)
+        dzfp = pool("dzfp", 3)
+        keep = pool("keep", 1)
+        cfp = pool("cfp", 6)
+        outp = pool("outp", 5)
+        psum = ctx.enter_context(tc.psum_pool(name="psum", bufs=8))
+
+        ident = const.tile([P, P], F32, name="ident")
+        make_identity(nc, ident[:])
+        warm = const.tile([P, 1], F32, name="warm")
+        V.memset(warm[:], 0.0)
+
+        ctx.enter_context(tc.manual_schedule())
+        S.activation(warm[:], warm[:], ACT.Sigmoid)
+
+        x_codes = [keep.tile([P, I], U32, name=f"xc{g}", align_bytes=64) for g in range(2)]
+        x_scales = [keep.tile([P, I], U8, name=f"xs{g}", align_bytes=64) for g in range(2)]
+        w_codes = [keep.tile([P, I], U32, name=f"wc{q}", align_bytes=64) for q in range(GATES)]
+        w_scales = [keep.tile([P, I], U8, name=f"ws{q}", align_bytes=64) for q in range(GATES)]
+        t_codes = {(g, q): keep.tile([P, H], U32, name=f"tc{g}{q}", align_bytes=64) for g in range(2) for q in range(GATES)}
+        t_scales = {(g, q): keep.tile([P, H], U8, name=f"ts{g}{q}", align_bytes=64) for g in range(2) for q in range(GATES)}
+        f_codes, f_scales = {}, {}
+        st = {}
+        bank_of = {}
+
+        def copy_op(eng):
+            return S.copy if eng == "S" else V.tensor_copy
+
+        def mult(out, a, b):
+            V.tensor_tensor(out=out, in0=a, in1=b, op=ALU.mult)
+
+        def minus_mult(out, a, b, k=1.0):
+            V.scalar_tensor_tensor(out=out, in0=a, scalar=k, in1=b, op0=ALU.subtract, op1=ALU.mult)
+
+        def quant(codes, scales, src, fmt):
+            V.quantize_mx(out=codes.bitcast(fmt), scales=scales, in_=src)
+
+        def il_copy(eng, dst, src):
+            copy_op(eng)(out=dst.rearrange("p (c i) t -> p c t i", i=4), in_=src.rearrange("p t (c i) -> p c t i", i=4))
+
+        def load(key, p, name, dt, width, src, cols=slice(None), new=True):
+            if new:
+                st[key] = p.tile([P, J, width], dt, name=name)
+            nc.sync.dma_start(out=st[key][:, :, cols], in_=src)
+
+        def zcols(q, s):
+            return slice(q * H + s.start, q * H + s.stop)
+
+        def act(key, func, scale=1.0, cols=slice(0, H)):
+            t = st[key][:, :, cols]
+            S.activation(t, t, func, scale=scale)
+
+        def both(f, out, a, b, **kw):
+            for s in halves:
+                f(st[out][:, :, s], st[a][:, :, s], st[b][:, :, s], **kw)
+
+        FIN = {3: ("z3", "cn"), 2: ("z2", "m"), 0: ("z0", "m"), 1: ("z1", "cn")}
+
+        def final(g, q, hw):
+            if ("dz", g, q) not in st:
+                shape = [P, J, H] if MODES[q] == "A" else [P, J, P, J]
+                st["dz", g, q] = dzp.tile(shape, BF16, name="dz", align_bytes=64)
+            dz, s = st["dz", g, q], halves[hw]
+            a, b = [st[k, g][:, :, s] for k in FIN[q]]
+            if MODES[q] == "A":
+                if q == 2:
+                    minus_mult(dz[:, :, s], a, b)
+                else:
+                    mult(dz[:, :, s], a, b)
+            else:
+                ms = slice(hw * 64, hw * 64 + 64)
+                mult(dz[:, :, ms, :].rearrange("p t m j -> p m j t"),
+                     a.rearrange("p j (m t) -> p m j t", t=J), b.rearrange("p j (m t) -> p m j t", t=J))
+
+        def transposes(g, q):
+            dz = st["dz", g, q]
+            banks = []
+            if MODES[q] == "A":
+                words = dz[:].rearrange("p j w -> p (j w)").bitcast(F32)
+            else:
+                words = dz[:].rearrange("p t m j -> p (t m j)").bitcast(F32)
+            for k in range(2):
+                bank = psum.tile([P, BANK], F32, name="bank")
+                banks.append(bank)
+                for n in range(4):
+                    if MODES[q] == "A":
+                        w0, u = (2 * k + n // 2) * HALF, n % 2
+                    else:
+                        w0, u = n * HALF, k
+                    T.transpose(bank[:, n * P:(n + 1) * P], words[:, w0 + u:w0 + HALF:2], ident[:])
+            st["tb", g, q] = banks
+            st["dzf", g, q] = None
+
+        def tcp(g, q, k, eng):
+            if st["dzf", g, q] is None:
+                st["dzf", g, q] = dzfp.tile([P, TOK * J], BF16, name="dzf", align_bytes=64)
+            dzf, bank = st["dzf", g, q], st["tb", g, q][k]
+            if MODES[q] == "A":
+                copy_op(eng)(out=dzf[:].bitcast(F32)[:, k * BANK:(k + 1) * BANK].rearrange("p (j r u) -> p j r u", j=2, u=2),
+                             in_=bank[:].rearrange("p (j u r) -> p j r u", j=2, u=2))
+            else:
+                copy_op(eng)(out=dzf[:, k * 1024:(k + 1) * 1024].rearrange("p (e r t) -> p e r t", e=2, t=J),
+                             in_=bank[:].bitcast(BF16).rearrange("p (t r e) -> p e r t", t=J, e=2))
+
+        def mm(bank, lc, ls, k, rc, rs, rcols, start, stop):
+            lcols = slice(k * P, (k + 1) * P)
+            T.matmul_mx(out=bank[:], lhsT=lc[:, lcols].bitcast(E5M2), lhsT_scale=ls[:, lcols],
+                        rhs=rc[:, rcols].bitcast(E4M3), rhs_scale=rs[:, rcols], start=start, stop=stop)
+
+        EARLY = [q for q in (3, 2, 0, 1) if q != LAST]
+
+        def o0(g, f, hw, gates, start, stop):
+            if start:
+                bank_of[0, g, f, hw] = psum.tile([P, BANK], F32, name="bank")
+            for n, q in enumerate(gates):
+                mm(bank_of[0, g, f, hw], f_codes[g, q], f_scales[g, q], f, w_codes[q], w_scales[q], wide[hw],
+                   start and n == 0, stop and n == len(gates) - 1)
+
+        def o1(q, f, hw):
+            bank_of[1, q, f, hw] = psum.tile([P, BANK], F32, name="bank")
+            for g in range(2):
+                mm(bank_of[1, q, f, hw], t_codes[g, q], t_scales[g, q], f, x_codes[g], x_scales[g], wide[hw], g == 0, g == 1)
+
+        def evac(o, a, f, hw, eng):
+            if ("ot", o, a, f) not in st:
+                st["ot", o, a, f] = outp.tile([P, I], F32, name="ot")
+            copy_op(eng)(out=st["ot", o, a, f][:, wide[hw]], in_=bank_of[o, a, f, hw][:])
+
+        def store(o, a, f):
+            if o == 0:
+                dst = tokens(out_0, a)[:, f, :]
+            elif MODES[a] == "A":
+                dst = out_1[a, f * P:(f + 1) * P, :]
+            else:
+                dst = out_1[a].rearrange("(m t) i -> m t i", t=J)[:, f, :]
+            nc.sync.dma_start(out=dst, in_=st["ot", o, a, f][:])
+
+        def step(s):
+            eng = "V"
+            if "/" in s:
+                s, eng = s.split("/")
+            if s.startswith("Lx"):
+                g = int(s[2])
+                if len(s) == 4:
+                    hw = int(s[3])
+                    load(("x", g), rawp, "raw", BF16, I, tokens(x, g, wide[hw]), wide[hw], new=("x", g) not in st)
+                else:
+                    load(("x", g), rawp, "raw", BF16, I, tokens(x, g))
+            elif s.startswith("Lw"):
+                q = int(s[2])
+                load(("w", q), rawp, "raw", BF16, I, Wx[q].rearrange("(p j) w -> p j w", j=J))
+            elif s.startswith("Lz"):
+                g, q = int(s[2]), int(s[3])
+                cols = slice(0, H) if len(s) == 4 else halves[0 if s[4] == "a" else 1]
+                load((f"z{q}", g), zp, "z", F32, H, tokens(z, g, zcols(q, cols)), cols, new=(f"z{q}", g) not in st)
+            elif s.startswith("Lcn"):
+                load(("cn", int(s[3])), cnp, "cn", F32, H, tokens(c_new, int(s[3])))
+            elif s.startswith("Lg"):
+                load((s[1:3], int(s[3])), in4, "in4", BF16, H, tokens(grad_0 if s[2] == "0" else grad_1, int(s[3])))
+            elif s.startswith("Lc"):
+                load(("c", int(s[2])), in4, "in4", BF16, H, tokens(c, int(s[2])))
+            elif s[1:3] == "il":
+                k, hw = int(s[3]), int(s[4])
+                st["il", s[0], k, hw] = ilp.tile([P, BANK, J], BF16, name="il", align_bytes=64)
+                il_copy(eng, st["il", s[0], k, hw][:], st[s[0], k][:, :, wide[hw]])
+            elif s[0] in "xw" and s[1] == "q" and len(s) == 4:
+                k, hw = int(s[2]), int(s[3])
+                codes, scales = (x_codes, x_scales) if s[0] == "x" else (w_codes, w_scales)
+                quant(codes[k][:, wide[hw]], scales[k][:, wide[hw]], st["il", s[0], k, hw][:].rearrange("p w t -> p (w t)"), E4M3)
+            elif s == "s3a0":
+                act(("z3", 0), ACT.Sigmoid, cols=halves[0])
+            elif s == "s30":
+                act(("z3", 0), ACT.Sigmoid, cols=halves[1])
+            elif s == "s31":
+                act(("z3", 1), ACT.Sigmoid)
+            elif s.startswith("s0"):
+                act(("z0", int(s[2])), ACT.Sigmoid)
+            elif s.startswith("t2"):
+                act(("z2", int(s[2])), ACT.Tanh)
+            elif s.startswith("t1"):
+                act(("z1", int(s[2])), ACT.Tanh, scale=0.5)
+            elif s.startswith("tc") and len(s) == 3:
+                act(("cn", int(s[2])), ACT.Tanh, scale=-1.0)
+            elif s.startswith("sqc"):
+                act(("cn", int(s[3])), ACT.Square)
+            elif s.startswith("sqg"):
+                act(("z2", int(s[3])), ACT.Square)
+            elif s.startswith("sq1"):
+                act(("z1", int(s[3])), ACT.Square, scale=0.5)
+            elif s[0] == "m":
+                g = int(s[1])
+                st["m", g] = mp.tile([P, J, H], F32, name="m")
+                both(mult, ("m", g), ("z3", g), ("g0", g))
+            elif s.startswith("a3"):
+                g = int(s[2])
+                both(minus_mult, ("z3", g), ("z3", g), ("m", g))
+            elif s.startswith("b0"):
+                g = int(s[2])
+                both(minus_mult, ("z0", g), ("z0", g), ("z2", g))
+            elif s.startswith("b1"):
+                g = int(s[2])
+                both(minus_mult, ("z1", g), ("z1", g), ("c", g), k=0.25)
+            elif s.startswith("x2"):
+                g = int(s[2])
+                both(mult, ("m", g), ("cn", g), ("z0", g))
+            elif s.startswith("ndc"):
+                g = int(s[3])
+                for hs in halves:
+                    V.tensor_tensor(out=st["cn", g][:, :, hs], in0=st["cn", g][:, :, hs], in1=st["g1", g][:, :, hs], op=ALU.subtract)
+            elif s.startswith("dz"):
+                final(int(s[3]), int(s[2]), "ab".index(s[4]))
+            elif s.startswith("il"):
+                g, q, hw = int(s[2]), int(s[3]), "ab".index(s[4])
+                if ("ilt", g, q) not in st:
+                    st["ilt", g, q] = ilp.tile([P, BANK, J], BF16, name="il", align_bytes=64)
+                il_copy(eng, st["ilt", g, q][:, halves[hw], :], st["dz", g, q][:, :, halves[hw]])
+            elif s.startswith("qt"):
+                g, q, hw = int(s[2]), int(s[3]), "ab".index(s[4])
+                if MODES[q] == "A":
+                    quant(t_codes[g, q][:, halves[hw]], t_scales[g, q][:, halves[hw]],
+                          st["ilt", g, q][:, halves[hw], :].rearrange("p w t -> p (w t)"), E5M2)
+                elif hw == 0:
+                    quant(t_codes[g, q][:], t_scales[g, q][:], st["dz", g, q][:].rearrange("p t m j -> p (t m j)"), E5M2)
+            elif s.startswith("qf"):
+                g, q = int(s[2]), int(s[3])
+                f_codes[g, q] = cfp.tile([P, TOK], U32, name="fc", align_bytes=64)
+                f_scales[g, q] = cfp.tile([P, TOK], U8, name="fs", align_bytes=64)
+                quant(f_codes[g, q][:], f_scales[g, q][:], st["dzf", g, q][:], E5M2)
+            elif s.startswith("tcp"):
+                tcp(int(s[3]), int(s[4]), "ab".index(s[5]), eng)
+            elif s[0] == "T":
+                transposes(int(s[1]), int(s[2]))
+            elif s.startswith("O0p"):
+                o0(int(s[3]), int(s[4]), int(s[5]), EARLY, True, False)
+            elif s.startswith("O0"):
+                o0(int(s[2]), int(s[3]), int(s[4]), [LAST], False, True)
+            elif s.startswith("O1"):
+                o1(int(s[2]), int(s[3]), int(s[4]))
+            elif s[0] == "e":
+                evac(int(s[1]), int(s[2]), int(s[3]), int(s[4]), eng)
+            elif s[0:2] == "st":
+                store(int(s[2]), int(s[3]), int(s[4]))
+            elif s[0] == "q":
+                g = int(s[1])
+                both(minus_mult, ("cn", g), ("cn", g), ("m", g))
+            else:
+                raise ValueError(s)
+
+        for name in STEPS:
+            step(name)

@@ -21,30 +21,31 @@ J = 4
 TOK = P * J
 BANK = 512
 HALF = H // 2
-MODES = "BBAB"
+MODES = "AAAA"
 LAST = 2
 STEPS = """
-Lx1 Lx01 Lz03a xil10/V xil11/S Lz03b xil01/V Lg00 s3a0 xq11 Lw0 xq10 xq01 s30
-m0 Lcn0 wil01/V wil00/S Lw1 a30 tc0 Lz13 wq00 wq01 wil11/V wil10/S Lg11 dz30a
-Lg01 s31 Lz11 wq11 wq10 dz30b m1 Lcn1 sqc0 T03 qt03a t11 Lc1 a31
-Lz02 tc1 q0 Lz10 sq11 dz31a qt03b Lx00 dz31b t20 Lw3 b11 T13 sqc1
-qt13a Lg10 tcp13a/V Lz00 tcp13b/S qt13b q1 wil31/S Lz12 qf13 ndc1 xil00/S Lc0 ndc0
-Lw2 wil30/S dz11a s01 wq30 xq00 wq31 O1300 dz11b O1330 t21 O1320 O1331 x21
-Lz01 T11 e1300/S e1331/S O1321 qt11a tcp11a/S O1301 b01 e1301/S O1310 wil21/S st130 O1311
-qt11b e1321/V dz01a sqg1 wq21 dz01b tcp11b/V e1310/S t10 T10 dz21a qf11 tcp10a/S dz21b
-il12a/V tcp10b/S T12 e1320/V sq10 qf10 st132 tcp12a/V O0p120 qt10a e1330/V O0p100 qt10b tcp12b/S
-st133 b10 O0p121 e1311/S wil20/S st131 O0p101 O0p130 qf12 dz10a O0121 O0101 s00 O0p131
-wq20 O0131 dz10b O0130 O0100 O0120 e0101/S e0100/V e0120/S O0p110 x20 st010 e0130/S T01
-e0131/S e0121/S st013 O0110 tcp03a/S O0p111 qt01a b00 st012 O1100 tcp01b/S O1110 O1101 e1100/S
-qt01b e1110/S O1111 dz00a e1101/S O1130 O0111 tcp01a/S st110 O1131 e1111/V O1120 dz00b e1130/S
-st111 e1131/S O1121 e0110/V e1120/S st113 T00 e1121/S e0111/V qt12a sqg0 st112 qt00a tcp00b/V
-O1000 st011 O1010 qt00b O1001 qf01 e1000/S O1011 dz20a e1010/S O1020 e1001/S O1030 dz20b
-e1011/S st100 O1021 e1020/S O1031 il02a/V tcp00a/S st101 T02 e1021/V e1031/S qt02a st102 qf00
-tcp03b/S O1210 tcp02a/V O1200 e1210/V il12b/S O1211 qf03 O1201 tcp02b/V O0p030 e1211/S e1201/V e1200/S
-st121 O0p010 qt12b qf02 O0p031 il02b/V st120 O0010 e1030/V O0p011 qt02b st103 e0010/V O0031
-O0011 O1230 e0031/S e0011/V O0030 O1231 e1230/V st001 e0030/S O0p020 e1231/S st003 O1220 O0020
-O1221 e1220/S st123 O0p021 e0020/S e1221/S O0p000 st122 O0021 O0p001 e0021/S O0000 st002 O0001
-e0000/V e0001/S st000
+Lw3 Lz03a Lx01 wil31/V wil30/S Lz03b wq31 Lg00 s3a0 xil01/V Lcn0a wq30 s30 Lcn0b
+xq01 m0 Lw1 tca0 tc0 a30 Lw2 wil10/V wil11/S Lc0 dz30a Lg10 wq10 wil21/S
+Lx11 dz30b Lz01 wq11 T03 wil20/V sqc0 tcp03a/V Lx00 wq20 wq21 tcp03b/S Lz00 q0
+xil11/S qf03 Lz02 t10 xq11 xil00/V ndc0 s00 Lz13 sq10 xq00 Lg01 x20 Lw0
+t20 b10 Lz11 s31 b00 Lg11 wil00/S m1 Lx10 Lc1 sqg0 dz10a Lcn1 dz00a
+il03a/S dz10b il00a/S qt03a T01 Lz12 il03b/V wq00 wil01/S qt03b dz20a qt00a dz20b tcp01b/S
+tc1 a31 T02 Lz10 t21 dz00b wq01 T00 il00b/V tcp02b/S xil10/V tcp02a/S tcp00a/S t11
+qt00b xq10 tcp00b/V qf02 qf00 tcp01a/S dz31a sq11 qf01 dz31b O0p010 il13a/S O0p020 b11
+sqc1 O0p030 O0p021 qt13a il01a/V O0p031 il13b/S q1 O0021 O1310 e0021/S O0p011 e1310/S st0021
+O1311 s01 qt01a O0011 qt13b O0p000 il01b/V ndc1 O0020 O0p001 e1311/S O0000 e0020/S O0001
+st131 O0030 e0000/S O0031 qt01b T13 dz11a e0030/S st0000 e0031/S st0020 e0011/S O0010 x21
+st0031 e0001/S st0030 O1330 e0010/S st0001 il11a/S O1331 st0010 dz11b O1320 st0011 e1331/S O1321
+e1330/V il11b/S O1300 qt11a st133 b01 O1100 e1300/S O1301 e1100/S O1110 e1301/S O1101 qt11b
+e1110/S st130 O1111 dz01a e1321/S O1120 e1101/S e1111/V T11 e1120/S st110 dz01b e1320/S O1121
+tcp11b/S st111 il10a/V T10 tcp11a/S e1121/V sqg1 st132 qt10a O1130 il10b/V O1010 qf11 st112
+O1131 qt10b il02a/V e1130/S O1030 e1131/S O1011 dz21a e1010/S st113 O1000 e1011/V tcp10a/S O1031
+e1030/S O1001 dz21b st101 tcp10b/S O1020 e1001/S e1031/V T12 il12a/V e1000/S st103 tcp13a/S qt02a
+O1021 qt12a tcp12b/S st100 tcp12a/V O1210 tcp13b/S qf10 O1200 e1210/S qf13 O1211 e1200/S e1020/V
+O1201 e1211/S il02b/V O0p120 e1201/S st121 e1021/V O0p110 qt02b qf12 st102 O0p121 il12b/V O0120
+O0p111 st120 qt12b e0120/V O0121 O0111 st0120 e0121/V O1220 O0110 e0111/V st0121 O1221 e1220/V
+st0111 O1230 e0110/V e1221/S O0p130 e1230/S st0110 O1231 st122 O0130 O0p131 e1231/S e0130/S st123
+O0p100 O0131 st0130 O0100 O0p101 e0131/S e0100/V st0131 O0101 st0100 e0101/V st0101
 """.split()
 
 
@@ -56,6 +57,7 @@ def tile_lstmcell_v_kernel(tc, x, h, c, Wx, Wh, bx, bh, z, c_new, grad_0, grad_1
         return t[g * TOK:(g + 1) * TOK, cols].rearrange("(p j) w -> p j w", j=J)
 
     halves = (slice(0, HALF), slice(HALF, H))
+    pairs = (slice(0, 2), slice(2, 4))
     wide = (slice(0, BANK), slice(BANK, 2 * BANK))
 
     with ExitStack() as ctx:
@@ -107,16 +109,13 @@ def tile_lstmcell_v_kernel(tc, x, h, c, Wx, Wh, bx, bh, z, c_new, grad_0, grad_1
         def il_copy(eng, dst, src):
             copy_op(eng)(out=dst.rearrange("p (c i) t -> p c t i", i=4), in_=src.rearrange("p t (c i) -> p c t i", i=4))
 
-        def load(key, p, name, dt, width, src, cols=slice(None), new=True):
+        def load(key, p, name, dt, width, src, js=slice(None), cols=slice(None), new=True):
             if new:
                 st[key] = p.tile([P, J, width], dt, name=name)
-            nc.sync.dma_start(out=st[key][:, :, cols], in_=src)
+            nc.sync.dma_start(out=st[key][:, js, cols], in_=src)
 
-        def zcols(q, s):
-            return slice(q * H + s.start, q * H + s.stop)
-
-        def act(key, func, scale=1.0, cols=slice(0, H)):
-            t = st[key][:, :, cols]
+        def act(key, func, scale=1.0, js=slice(0, J)):
+            t = st[key][:, js, :]
             S.activation(t, t, func, scale=scale)
 
         def both(f, out, a, b, **kw):
@@ -195,7 +194,10 @@ def tile_lstmcell_v_kernel(tc, x, h, c, Wx, Wh, bx, bh, z, c_new, grad_0, grad_1
                 st["ot", o, a, f] = outp.tile([P, I], F32, name="ot")
             copy_op(eng)(out=st["ot", o, a, f][:, wide[hw]], in_=bank_of[o, a, f, hw][:])
 
-        def store(o, a, f):
+        def store(o, a, f, hw=None):
+            if hw is not None:
+                nc.sync.dma_start(out=tokens(out_0, a, wide[hw])[:, f, :], in_=st["ot", o, a, f][:, wide[hw]])
+                return
             if o == 0:
                 dst = tokens(out_0, a)[:, f, :]
             elif MODES[a] == "A":
@@ -210,20 +212,19 @@ def tile_lstmcell_v_kernel(tc, x, h, c, Wx, Wh, bx, bh, z, c_new, grad_0, grad_1
                 s, eng = s.split("/")
             if s.startswith("Lx"):
                 g = int(s[2])
-                if len(s) == 4:
-                    hw = int(s[3])
-                    load(("x", g), rawp, "raw", BF16, I, tokens(x, g, wide[hw]), wide[hw], new=("x", g) not in st)
-                else:
-                    load(("x", g), rawp, "raw", BF16, I, tokens(x, g))
+                hw = int(s[3])
+                load(("x", g), rawp, "raw", BF16, I, tokens(x, g, wide[hw]), cols=wide[hw], new=("x", g) not in st)
             elif s.startswith("Lw"):
                 q = int(s[2])
                 load(("w", q), rawp, "raw", BF16, I, Wx[q].rearrange("(p j) w -> p j w", j=J))
             elif s.startswith("Lz"):
                 g, q = int(s[2]), int(s[3])
-                cols = slice(0, H) if len(s) == 4 else halves[0 if s[4] == "a" else 1]
-                load((f"z{q}", g), zp, "z", F32, H, tokens(z, g, zcols(q, cols)), cols, new=(f"z{q}", g) not in st)
+                js = slice(0, J) if len(s) == 4 else pairs["ab".index(s[4])]
+                load((f"z{q}", g), zp, "z", F32, H, tokens(z, g, slice(q * H, (q + 1) * H))[:, js, :], js, new=(f"z{q}", g) not in st)
             elif s.startswith("Lcn"):
-                load(("cn", int(s[3])), cnp, "cn", F32, H, tokens(c_new, int(s[3])))
+                g = int(s[3])
+                js = slice(0, J) if len(s) == 4 else pairs["ab".index(s[4])]
+                load(("cn", g), cnp, "cn", F32, H, tokens(c_new, g)[:, js, :], js, new=("cn", g) not in st)
             elif s.startswith("Lg"):
                 load((s[1:3], int(s[3])), in4, "in4", BF16, H, tokens(grad_0 if s[2] == "0" else grad_1, int(s[3])))
             elif s.startswith("Lc"):
@@ -237,9 +238,9 @@ def tile_lstmcell_v_kernel(tc, x, h, c, Wx, Wh, bx, bh, z, c_new, grad_0, grad_1
                 codes, scales = (x_codes, x_scales) if s[0] == "x" else (w_codes, w_scales)
                 quant(codes[k][:, wide[hw]], scales[k][:, wide[hw]], st["il", s[0], k, hw][:].rearrange("p w t -> p (w t)"), E4M3)
             elif s == "s3a0":
-                act(("z3", 0), ACT.Sigmoid, cols=halves[0])
+                act(("z3", 0), ACT.Sigmoid, js=pairs[0])
             elif s == "s30":
-                act(("z3", 0), ACT.Sigmoid, cols=halves[1])
+                act(("z3", 0), ACT.Sigmoid, js=pairs[1])
             elif s == "s31":
                 act(("z3", 1), ACT.Sigmoid)
             elif s.startswith("s0"):
@@ -248,8 +249,12 @@ def tile_lstmcell_v_kernel(tc, x, h, c, Wx, Wh, bx, bh, z, c_new, grad_0, grad_1
                 act(("z2", int(s[2])), ACT.Tanh)
             elif s.startswith("t1"):
                 act(("z1", int(s[2])), ACT.Tanh, scale=0.5)
-            elif s.startswith("tc") and len(s) == 3:
-                act(("cn", int(s[2])), ACT.Tanh, scale=-1.0)
+            elif s == "tca0":
+                act(("cn", 0), ACT.Tanh, scale=-1.0, js=pairs[0])
+            elif s == "tc0":
+                act(("cn", 0), ACT.Tanh, scale=-1.0, js=pairs[1])
+            elif s == "tc1":
+                act(("cn", 1), ACT.Tanh, scale=-1.0)
             elif s.startswith("sqc"):
                 act(("cn", int(s[3])), ACT.Square)
             elif s.startswith("sqg"):
@@ -308,7 +313,7 @@ def tile_lstmcell_v_kernel(tc, x, h, c, Wx, Wh, bx, bh, z, c_new, grad_0, grad_1
             elif s[0] == "e":
                 evac(int(s[1]), int(s[2]), int(s[3]), int(s[4]), eng)
             elif s[0:2] == "st":
-                store(int(s[2]), int(s[3]), int(s[4]))
+                store(int(s[2]), int(s[3]), int(s[4]), int(s[5]) if len(s) == 6 else None)
             elif s[0] == "q":
                 g = int(s[1])
                 both(minus_mult, ("cn", g), ("cn", g), ("m", g))

from contextlib import ExitStack

import concourse.mybir as mybir
from concourse.masks import make_identity

B, I, H, GATES = 1024, 1024, 512, 4
FLOPS = 2 * 2 * B * GATES * H * I
BYTES = 2 * (B * I + B * H + GATES * H * I + 2 * B * H) + 4 * (B * GATES * H + B * H) + 4 * (B * I + GATES * H * I)

F32 = mybir.dt.float32
BF16 = mybir.dt.bfloat16
U32 = mybir.dt.uint32
U8 = mybir.dt.uint8
E4M3 = mybir.dt.float8_e4m3fn_x4
E5M2 = mybir.dt.float8_e5m2_x4
ACT = mybir.ActivationFunctionType
ALU = mybir.AluOpType

P = 128
J = 4
TOK = P * J
BANK = 512
HALF = H // 2
MODES = "AAAA"
LAST = 2
STEPS = """
Lw3 Lz03a Lx01 wil31/V wil30/S Lz03b wq31 Lg00 s3a0 xil01/V Lcn0a wq30 s30 Lcn0b
xq01 m0 Lw1 tca0 tc0 a30 Lw2 wil10/V wil11/S Lc0 dz30a Lg10 wq10 wil21/S
Lx11 dz30b Lz01 wq11 T03 wil20/V sqc0 tcp03a/V Lx00 wq20 wq21 tcp03b/S Lz00 q0
xil11/S qf03 Lz02 t10 xq11 xil00/V ndc0 s00 Lz13 sq10 xq00 Lg01 x20 Lw0
t20 b10 Lz11 s31 b00 Lg11 wil00/S m1 Lx10 Lc1 sqg0 dz10a Lcn1 dz00a
il03a/S dz10b il00a/S qt03a T01 Lz12 il03b/V wq00 wil01/S qt03b dz20a qt00a dz20b tcp01b/S
tc1 a31 T02 Lz10 t21 dz00b wq01 T00 il00b/V tcp02b/S xil10/V tcp02a/S tcp00a/S t11
qt00b xq10 tcp00b/V qf02 qf00 tcp01a/S dz31a sq11 qf01 dz31b O0p010 il13a/S O0p020 b11
sqc1 O0p030 O0p021 qt13a il01a/V O0p031 il13b/S q1 O0021 O1310 e0021/S O0p011 e1310/S st0021
O1311 s01 qt01a O0011 qt13b O0p000 il01b/V ndc1 O0020 O0p001 e1311/S O0000 e0020/S O0001
st131 O0030 e0000/S O0031 qt01b T13 dz11a e0030/S st0000 e0031/S st0020 e0011/S O0010 x21
st0031 e0001/S st0030 O1330 e0010/S st0001 il11a/S O1331 st0010 dz11b O1320 st0011 e1331/S O1321
e1330/V il11b/S O1300 qt11a st133 b01 O1100 e1300/S O1301 e1100/S O1110 e1301/S O1101 qt11b
e1110/S st130 O1111 dz01a e1321/S O1120 e1101/S e1111/V T11 e1120/S st110 dz01b e1320/S O1121
tcp11b/S st111 il10a/V T10 tcp11a/S e1121/V sqg1 st132 qt10a O1130 il10b/V O1010 qf11 st112
O1131 qt10b il02a/V e1130/S O1030 e1131/S O1011 dz21a e1010/S st113 O1000 e1011/V tcp10a/S O1031
e1030/S O1001 dz21b st101 tcp10b/S O1020 e1001/S e1031/V T12 il12a/V e1000/S st103 tcp13a/S qt02a
O1021 qt12a tcp12b/S st100 tcp12a/V O1210 tcp13b/S qf10 O1200 e1210/S qf13 O1211 e1200/S e1020/V
O1201 e1211/S il02b/V O0p120 e1201/S st121 e1021/V O0p110 qt02b qf12 st102 O0p121 il12b/V O0120
O0p111 st120 qt12b e0120/V O0121 O0111 st0120 e0121/V O1220 O0110 e0111/V st0121 O1221 e1220/V
st0111 O1230 e0110/V e1221/S O0p130 e1230/S st0110 O1231 st122 O0130 O0p131 e1231/S e0130/S st123
O0p100 O0131 st0130 O0100 O0p101 e0131/S e0100/V st0131 O0101 st0100 e0101/V st0101
""".split()


def tile_lstmcell_v_kernel(tc, x, h, c, Wx, Wh, bx, bh, z, c_new, grad_0, grad_1, out_0, out_1):
    nc = tc.nc
    V, S, T = nc.vector, nc.scalar, nc.tensor

    def tokens(t, g, cols=slice(None)):
        return t[g * TOK:(g + 1) * TOK, cols].rearrange("(p j) w -> p j w", j=J)

    halves = (slice(0, HALF), slice(HALF, H))
    pairs = (slice(0, 2), slice(2, 4))
    wide = (slice(0, BANK), slice(BANK, 2 * BANK))

    with ExitStack() as ctx:
        pool = lambda name, bufs: ctx.enter_context(tc.tile_pool(name=name, bufs=bufs))
        const = pool("const", 1)
        zp = pool("zp", 5)
        cnp = pool("cnp", 2)
        rawp = pool("rawp", 3)
        mp = pool("mp", 2)
        in4 = pool("in4", 4)
        dzp = pool("dzp", 3)
        ilp = pool("ilp", 4)
        dzfp = pool("dzfp", 3)
        keep = pool("keep", 1)
        cfp = pool("cfp", 6)
        outp = pool("outp", 5)
        psum = ctx.enter_context(tc.psum_pool(name="psum", bufs=8))

        ident = const.tile([P, P], F32, name="ident")
        make_identity(nc, ident[:])
        warm = const.tile([P, 1], F32, name="warm")
        V.memset(warm[:], 0.0)

        ctx.enter_context(tc.manual_schedule())
        S.activation(warm[:], warm[:], ACT.Sigmoid)

        x_codes = [keep.tile([P, I], U32, name=f"xc{g}", align_bytes=64) for g in range(2)]
        x_scales = [keep.tile([P, I], U8, name=f"xs{g}", align_bytes=64) for g in range(2)]
        w_codes = [keep.tile([P, I], U32, name=f"wc{q}", align_bytes=64) for q in range(GATES)]
        w_scales = [keep.tile([P, I], U8, name=f"ws{q}", align_bytes=64) for q in range(GATES)]
        t_codes = {(g, q): keep.tile([P, H], U32, name=f"tc{g}{q}", align_bytes=64) for g in range(2) for q in range(GATES)}
        t_scales = {(g, q): keep.tile([P, H], U8, name=f"ts{g}{q}", align_bytes=64) for g in range(2) for q in range(GATES)}
        f_codes, f_scales = {}, {}
        st = {}
        bank_of = {}

        def copy_op(eng):
            return S.copy if eng == "S" else V.tensor_copy

        def mult(out, a, b):
            V.tensor_tensor(out=out, in0=a, in1=b, op=ALU.mult)

        def minus_mult(out, a, b, k=1.0):
            V.scalar_tensor_tensor(out=out, in0=a, scalar=k, in1=b, op0=ALU.subtract, op1=ALU.mult)

        def quant(codes, scales, src, fmt):
            V.quantize_mx(out=codes.bitcast(fmt), scales=scales, in_=src)

        def il_copy(eng, dst, src):
            copy_op(eng)(out=dst.rearrange("p (c i) t -> p c t i", i=4), in_=src.rearrange("p t (c i) -> p c t i", i=4))

        def load(key, p, name, dt, width, src, js=slice(None), cols=slice(None), new=True):
            if new:
                st[key] = p.tile([P, J, width], dt, name=name)
            nc.sync.dma_start(out=st[key][:, js, cols], in_=src)

        def act(key, func, scale=1.0, js=slice(0, J)):
            t = st[key][:, js, :]
            S.activation(t, t, func, scale=scale)

        def both(f, out, a, b, **kw):
            for s in halves:
                f(st[out][:, :, s], st[a][:, :, s], st[b][:, :, s], **kw)

        FIN = {3: ("z3", "cn"), 2: ("z2", "m"), 0: ("z0", "m"), 1: ("z1", "cn")}

        def final(g, q, hw):
            if ("dz", g, q) not in st:
                shape = [P, J, H] if MODES[q] == "A" else [P, J, P, J]
                st["dz", g, q] = dzp.tile(shape, BF16, name="dz", align_bytes=64)
            dz, s = st["dz", g, q], halves[hw]
            a, b = [st[k, g][:, :, s] for k in FIN[q]]
            if MODES[q] == "A":
                if q == 2:
                    minus_mult(dz[:, :, s], a, b)
                else:
                    mult(dz[:, :, s], a, b)
            else:
                ms = slice(hw * 64, hw * 64 + 64)
                mult(dz[:, :, ms, :].rearrange("p t m j -> p m j t"),
                     a.rearrange("p j (m t) -> p m j t", t=J), b.rearrange("p j (m t) -> p m j t", t=J))

        def transposes(g, q):
            dz = st["dz", g, q]
            banks = []
            if MODES[q] == "A":
                words = dz[:].rearrange("p j w -> p (j w)").bitcast(F32)
            else:
                words = dz[:].rearrange("p t m j -> p (t m j)").bitcast(F32)
            for k in range(2):
                bank = psum.tile([P, BANK], F32, name="bank")
                banks.append(bank)
                for n in range(4):
                    if MODES[q] == "A":
                        w0, u = (2 * k + n // 2) * HALF, n % 2
                    else:
                        w0, u = n * HALF, k
                    T.transpose(bank[:, n * P:(n + 1) * P], words[:, w0 + u:w0 + HALF:2], ident[:])
            st["tb", g, q] = banks
            st["dzf", g, q] = None

        def tcp(g, q, k, eng):
            if st["dzf", g, q] is None:
                st["dzf", g, q] = dzfp.tile([P, TOK * J], BF16, name="dzf", align_bytes=64)
            dzf, bank = st["dzf", g, q], st["tb", g, q][k]
            if MODES[q] == "A":
                copy_op(eng)(out=dzf[:].bitcast(F32)[:, k * BANK:(k + 1) * BANK].rearrange("p (j r u) -> p j r u", j=2, u=2),
                             in_=bank[:].rearrange("p (j u r) -> p j r u", j=2, u=2))
            else:
                copy_op(eng)(out=dzf[:, k * 1024:(k + 1) * 1024].rearrange("p (e r t) -> p e r t", e=2, t=J),
                             in_=bank[:].bitcast(BF16).rearrange("p (t r e) -> p e r t", t=J, e=2))

        def mm(bank, lc, ls, k, rc, rs, rcols, start, stop):
            lcols = slice(k * P, (k + 1) * P)
            T.matmul_mx(out=bank[:], lhsT=lc[:, lcols].bitcast(E5M2), lhsT_scale=ls[:, lcols],
                        rhs=rc[:, rcols].bitcast(E4M3), rhs_scale=rs[:, rcols], start=start, stop=stop)

        EARLY = [q for q in (3, 2, 0, 1) if q != LAST]

        def o0(g, f, hw, gates, start, stop):
            if start:
                bank_of[0, g, f, hw] = psum.tile([P, BANK], F32, name="bank")
            for n, q in enumerate(gates):
                mm(bank_of[0, g, f, hw], f_codes[g, q], f_scales[g, q], f, w_codes[q], w_scales[q], wide[hw],
                   start and n == 0, stop and n == len(gates) - 1)

        def o1(q, f, hw):
            bank_of[1, q, f, hw] = psum.tile([P, BANK], F32, name="bank")
            for g in range(2):
                mm(bank_of[1, q, f, hw], t_codes[g, q], t_scales[g, q], f, x_codes[g], x_scales[g], wide[hw], g == 0, g == 1)

        def evac(o, a, f, hw, eng):
            if ("ot", o, a, f) not in st:
                st["ot", o, a, f] = outp.tile([P, I], F32, name="ot")
            copy_op(eng)(out=st["ot", o, a, f][:, wide[hw]], in_=bank_of[o, a, f, hw][:])

        def store(o, a, f, hw=None):
            if hw is not None:
                nc.sync.dma_start(out=tokens(out_0, a, wide[hw])[:, f, :], in_=st["ot", o, a, f][:, wide[hw]])
                return
            if o == 0:
                dst = tokens(out_0, a)[:, f, :]
            elif MODES[a] == "A":
                dst = out_1[a, f * P:(f + 1) * P, :]
            else:
                dst = out_1[a].rearrange("(m t) i -> m t i", t=J)[:, f, :]
            nc.sync.dma_start(out=dst, in_=st["ot", o, a, f][:])

        def step(s):
            eng = "V"
            if "/" in s:
                s, eng = s.split("/")
            if s.startswith("Lx"):
                g = int(s[2])
                hw = int(s[3])
                load(("x", g), rawp, "raw", BF16, I, tokens(x, g, wide[hw]), cols=wide[hw], new=("x", g) not in st)
            elif s.startswith("Lw"):
                q = int(s[2])
                load(("w", q), rawp, "raw", BF16, I, Wx[q].rearrange("(p j) w -> p j w", j=J))
            elif s.startswith("Lz"):
                g, q = int(s[2]), int(s[3])
                js = slice(0, J) if len(s) == 4 else pairs["ab".index(s[4])]
                load((f"z{q}", g), zp, "z", F32, H, tokens(z, g, slice(q * H, (q + 1) * H))[:, js, :], js, new=(f"z{q}", g) not in st)
            elif s.startswith("Lcn"):
                g = int(s[3])
                js = slice(0, J) if len(s) == 4 else pairs["ab".index(s[4])]
                load(("cn", g), cnp, "cn", F32, H, tokens(c_new, g)[:, js, :], js, new=("cn", g) not in st)
            elif s.startswith("Lg"):
                load((s[1:3], int(s[3])), in4, "in4", BF16, H, tokens(grad_0 if s[2] == "0" else grad_1, int(s[3])))
            elif s.startswith("Lc"):
                load(("c", int(s[2])), in4, "in4", BF16, H, tokens(c, int(s[2])))
            elif s[1:3] == "il":
                k, hw = int(s[3]), int(s[4])
                st["il", s[0], k, hw] = ilp.tile([P, BANK, J], BF16, name="il", align_bytes=64)
                il_copy(eng, st["il", s[0], k, hw][:], st[s[0], k][:, :, wide[hw]])
            elif s[0] in "xw" and s[1] == "q" and len(s) == 4:
                k, hw = int(s[2]), int(s[3])
                codes, scales = (x_codes, x_scales) if s[0] == "x" else (w_codes, w_scales)
                quant(codes[k][:, wide[hw]], scales[k][:, wide[hw]], st["il", s[0], k, hw][:].rearrange("p w t -> p (w t)"), E4M3)
            elif s == "s3a0":
                act(("z3", 0), ACT.Sigmoid, js=pairs[0])
            elif s == "s30":
                act(("z3", 0), ACT.Sigmoid, js=pairs[1])
            elif s == "s31":
                act(("z3", 1), ACT.Sigmoid)
            elif s.startswith("s0"):
                act(("z0", int(s[2])), ACT.Sigmoid)
            elif s.startswith("t2"):
                act(("z2", int(s[2])), ACT.Tanh)
            elif s.startswith("t1"):
                act(("z1", int(s[2])), ACT.Tanh, scale=0.5)
            elif s == "tca0":
                act(("cn", 0), ACT.Tanh, scale=-1.0, js=pairs[0])
            elif s == "tc0":
                act(("cn", 0), ACT.Tanh, scale=-1.0, js=pairs[1])
            elif s == "tc1":
                act(("cn", 1), ACT.Tanh, scale=-1.0)
            elif s.startswith("sqc"):
                act(("cn", int(s[3])), ACT.Square)
            elif s.startswith("sqg"):
                act(("z2", int(s[3])), ACT.Square)
            elif s.startswith("sq1"):
                act(("z1", int(s[3])), ACT.Square, scale=0.5)
            elif s[0] == "m":
                g = int(s[1])
                st["m", g] = mp.tile([P, J, H], F32, name="m")
                both(mult, ("m", g), ("z3", g), ("g0", g))
            elif s.startswith("a3"):
                g = int(s[2])
                both(minus_mult, ("z3", g), ("z3", g), ("m", g))
            elif s.startswith("b0"):
                g = int(s[2])
                both(minus_mult, ("z0", g), ("z0", g), ("z2", g))
            elif s.startswith("b1"):
                g = int(s[2])
                both(minus_mult, ("z1", g), ("z1", g), ("c", g), k=0.25)
            elif s.startswith("x2"):
                g = int(s[2])
                both(mult, ("m", g), ("cn", g), ("z0", g))
            elif s.startswith("ndc"):
                g = int(s[3])
                for hs in halves:
                    V.tensor_tensor(out=st["cn", g][:, :, hs], in0=st["cn", g][:, :, hs], in1=st["g1", g][:, :, hs], op=ALU.subtract)
            elif s.startswith("dz"):
                final(int(s[3]), int(s[2]), "ab".index(s[4]))
            elif s.startswith("il"):
                g, q, hw = int(s[2]), int(s[3]), "ab".index(s[4])
                if ("ilt", g, q) not in st:
                    st["ilt", g, q] = ilp.tile([P, BANK, J], BF16, name="il", align_bytes=64)
                il_copy(eng, st["ilt", g, q][:, halves[hw], :], st["dz", g, q][:, :, halves[hw]])
            elif s.startswith("qt"):
                g, q, hw = int(s[2]), int(s[3]), "ab".index(s[4])
                if MODES[q] == "A":
                    quant(t_codes[g, q][:, halves[hw]], t_scales[g, q][:, halves[hw]],
                          st["ilt", g, q][:, halves[hw], :].rearrange("p w t -> p (w t)"), E5M2)
                elif hw == 0:
                    quant(t_codes[g, q][:], t_scales[g, q][:], st["dz", g, q][:].rearrange("p t m j -> p (t m j)"), E5M2)
            elif s.startswith("qf"):
                g, q = int(s[2]), int(s[3])
                f_codes[g, q] = cfp.tile([P, TOK], U32, name="fc", align_bytes=64)
                f_scales[g, q] = cfp.tile([P, TOK], U8, name="fs", align_bytes=64)
                quant(f_codes[g, q][:], f_scales[g, q][:], st["dzf", g, q][:], E5M2)
            elif s.startswith("tcp"):
                tcp(int(s[3]), int(s[4]), "ab".index(s[5]), eng)
            elif s[0] == "T":
                transposes(int(s[1]), int(s[2]))
            elif s.startswith("O0p"):
                o0(int(s[3]), int(s[4]), int(s[5]), EARLY, True, False)
            elif s.startswith("O0"):
                o0(int(s[2]), int(s[3]), int(s[4]), [LAST], False, True)
            elif s.startswith("O1"):
                o1(int(s[2]), int(s[3]), int(s[4]))
            elif s[0] == "e":
                evac(int(s[1]), int(s[2]), int(s[3]), int(s[4]), eng)
            elif s[0:2] == "st":
                store(int(s[2]), int(s[3]), int(s[4]), int(s[5]) if len(s) == 6 else None)
            elif s[0] == "q":
                g = int(s[1])
                both(minus_mult, ("cn", g), ("cn", g), ("m", g))
            else:
                raise ValueError(s)

        for name in STEPS:
            step(name)
